import numpy as np
import ml_dtypes


def mxq(x, axis, fmt="e4m3"):
    dtype, down = {"e4m3": (ml_dtypes.float8_e4m3fn, 7), "e5m2": (ml_dtypes.float8_e5m2, 14)}[fmt]
    v = np.moveaxis(np.asarray(x, np.float32).astype(ml_dtypes.bfloat16).astype(np.float64), axis, -1)
    blocks = v.reshape(v.shape[:-1] + (-1, 32))
    amax = np.abs(blocks).max(-1, keepdims=True)
    byte = np.maximum(np.where(amax > 0, np.frexp(amax)[1] - 1 + 127, 0) - down, 1)
    scale = np.exp2(byte - 127.0)
    codes = (blocks / scale).astype(np.float32).astype(dtype).astype(np.float64)
    return np.moveaxis((codes * scale).reshape(v.shape), -1, axis)


WIDE = False


def mx_kscale(k):
    if not WIDE:
        return np.ones(k)
    levels = np.array([20, -20, 10, -10, 0])
    a = np.random.permutation(np.resize(levels, k // 512 * 4)).reshape(k // 512, 4)
    idx = np.arange(k)
    return np.exp2(a[idx // 512, idx % 128 // 32])


BF16 = ml_dtypes.bfloat16


def bf(x):
    return np.asarray(x, np.float32).astype(BF16)


def f64(x):
    return np.asarray(x).astype(np.float64)


B, N, F, O, E, K = 4, 512, 512, 64, 16, 3


def setup_inputs():
    se = np.asarray(mx_kscale(E * O)).reshape(E, O)[:, 0]
    x_g = np.random.standard_normal((B, K, N, F))
    emb = np.random.standard_normal((B, N, E)) * se
    weights_pool = np.random.standard_normal((E, K, F, O)) * 0.5 / np.sqrt(K * F) / se[:, None, None, None]
    bias_pool = np.random.standard_normal((E, O)) * 0.3 / se[:, None]
    g = np.random.standard_normal((B, N, O)) * np.exp2(np.random.randint(-12, 1, (B, N, 1))) * 64.0
    return {"x_g": bf(x_g), "emb": bf(emb), "weights_pool": bf(weights_pool), "bias_pool": bf(bias_pool),
            "grad_out": bf(g)}


def reference(x_g, emb, weights_pool, bias_pool, grad_out):
    e, w, g = f64(emb), f64(weights_pool), f64(grad_out)
    gz = (e[:, :, :, None] * g[:, :, None, :]).reshape(B * N, E * O)
    wt = w.transpose(1, 2, 0, 3).reshape(K * F, E * O)
    gx = mxq(gz, 1, "e5m2") @ mxq(wt, 1, "e4m3").T
    return gx.reshape(B, N, K, F).transpose(0, 2, 1, 3)

@@ -1,0 +1,177 @@
+from contextlib import ExitStack
+
+import concourse.mybir as mybir
+from concourse.masks import make_identity
+
+BF16 = mybir.dt.bfloat16
+F32 = mybir.dt.float32
+U32 = mybir.dt.uint32
+U8 = mybir.dt.uint8
+E4M3_X4 = mybir.dt.float8_e4m3fn_x4
+E5M2_X4 = mybir.dt.float8_e5m2_x4
+
+B, N, F, O, E, K = 4, 512, 512, 64, 16, 3
+P = 128
+PACK = 4
+PASSES = E * O // (P * PACK)
+E_PASS = E // PASSES
+TOKEN_TILES = B * N // P
+TILES_PER_BATCH = N // P
+CHUNK_TILES = 4
+CHUNK = CHUNK_TILES * P
+F_ROWS = F // P
+
+SKEW = 2
+AHEAD = 2
+VECTOR_TURN = 6
+
+FLOPS = 2 * B * N * K * F * E * O
+BYTES = 2 * (B * N * E + B * N * O + E * K * F * O) + 4 * B * K * N * F
+
+
+def tile_dygcn_pb_kernel(tc, x_g, emb, weights_pool, bias_pool, grad_out, out):
+    nc = tc.nc
+    mult = mybir.AluOpType.mult
+
+    with ExitStack() as stack:
+        const = stack.enter_context(tc.tile_pool(name="const", bufs=1))
+        keep = stack.enter_context(tc.tile_pool(name="keep", bufs=1))
+        work = stack.enter_context(tc.tile_pool(name="work", bufs=2))
+        results = stack.enter_context(tc.tile_pool(name="results", bufs=8))
+        psum_bank = stack.enter_context(tc.psum_pool(name="psum_bank", bufs=4))
+        psum_g = stack.enter_context(tc.psum_pool(name="psum_g", bufs=2))
+        psum_tok = stack.enter_context(tc.psum_pool(name="psum_tok", bufs=2))
+
+        tok_rows = keep.tile([P, TOKEN_TILES, P], BF16)
+        nc.vector.memset(tok_rows[:, :, O + E :], 0.0)
+        nc.scalar.dma_start(out=tok_rows[:, :, 0:O], in_=grad_out.rearrange("b (i p) o -> p (b i) o", p=P))
+        nc.scalar.dma_start(out=tok_rows[:, :, O : O + E], in_=emb.rearrange("b (i p) e -> p (b i) e", p=P))
+
+        w_raw = keep.tile([P, K, E, F_ROWS * O], BF16)
+        for k in range(K):
+            for h in range(PASSES):
+                e_range = slice(h * E_PASS, (h + 1) * E_PASS)
+                nc.sync.dma_start(
+                    out=w_raw[:, k, e_range, :],
+                    in_=weights_pool[e_range, k].rearrange("e (p j) o -> p e (j o)", j=F_ROWS),
+                )
+
+        ident_bf16 = const.tile([P, P], BF16)
+        make_identity(nc, ident_bf16[:])
+        ident_f32 = const.tile([P, P], F32)
+        make_identity(nc, ident_f32[:])
+
+        select_o = const.tile([P, PACK, P], BF16)
+        ident_by_o = ident_bf16[:, 0:O].rearrange("r (a u q s) -> r u s a q", a=2, u=2, q=8)
+        for u in range(2):
+            for s in range(2):
+                nc.vector.tensor_copy(
+                    out=select_o[:, 2 * u + s, :].rearrange("r (e a q) -> r e a q", e=E_PASS, a=2),
+                    in_=ident_by_o[:, u, s].unsqueeze(1).to_broadcast([P, E_PASS, 2, 8]),
+                )
+        select_e = const.tile([P, PASSES, P], BF16)
+        for h in range(PASSES):
+            first = O + h * E_PASS
+            nc.vector.tensor_copy(
+                out=select_e[:, h, :].rearrange("r (e x) -> r e x", e=E_PASS),
+                in_=ident_bf16[:, first : first + E_PASS].unsqueeze(2).to_broadcast([P, E_PASS, P // E_PASS]),
+            )
+
+        tok_cols = keep.tile([P, TOKEN_TILES * P], BF16)
+        emb_spread = keep.tile([P, PASSES, TOKEN_TILES * P], BF16)
+        for chunk in range(TOKEN_TILES // CHUNK_TILES):
+            cols = slice(chunk * CHUNK, (chunk + 1) * CHUNK)
+            flipped = psum_tok.tile([P, CHUNK_TILES, P], BF16, tag="tok")
+            for i in range(CHUNK_TILES):
+                nc.tensor.transpose(flipped[:, i, :], tok_rows[:, chunk * CHUNK_TILES + i, :], ident_bf16[:])
+            nc.scalar.copy(out=tok_cols[:, cols], in_=flipped[:].rearrange("r i p -> r (i p)"))
+            spread = psum_tok.tile([P, PASSES, CHUNK], BF16, tag="tok")
+            for h in range(PASSES):
+                nc.tensor.matmul(
+                    out=spread[:, h, :], lhsT=select_e[:, h, :], rhs=tok_cols[:, cols], start=True, stop=True
+                )
+            nc.scalar.copy(out=emb_spread[:, :, cols], in_=spread[:])
+
+        gz_codes = keep.tile([P, TOKEN_TILES, PASSES * P], U32, align_bytes=64)
+        gz_scales = keep.tile([P, TOKEN_TILES, PASSES * P], U8, align_bytes=64)
+        w_codes = keep.tile([P, K, PASSES, F], U32, align_bytes=64)
+        w_scales = keep.tile([P, K, PASSES, F], U8, align_bytes=64)
+
+        def quantise_gz(i):
+            cols = slice(i * P, (i + 1) * P)
+            g_spread = psum_g.tile([P, PACK, P], F32, tag="g")
+            for t in range(PACK):
+                nc.tensor.matmul(
+                    out=g_spread[:, t, :], lhsT=select_o[:, t, :], rhs=tok_cols[:, cols], start=True, stop=True
+                )
+            gz = work.tile([P, PASSES, P, PACK], BF16, align_bytes=64, bufs=3)
+            nc.vector.tensor_tensor(
+                out=gz[:],
+                in0=g_spread[:].rearrange("c t n -> c n t").unsqueeze(1).to_broadcast([P, PASSES, P, PACK]),
+                in1=emb_spread[:, :, cols].unsqueeze(3).to_broadcast([P, PASSES, P, PACK]),
+                op=mult,
+            )
+            nc.vector.quantize_mx(
+                out=gz_codes[:, i, :].bitcast(E5M2_X4),
+                scales=gz_scales[:, i, :],
+                in_=gz[:].rearrange("c h n t -> c (h n t)"),
+            )
+
+        def quantise_weights(k):
+            w_sorted = work.tile([P, PASSES, F_ROWS, 2, 2 * P], BF16)
+            raw_view = w_raw[:, k].rearrange("p (h e) (j a u x) -> p h u j e a x", h=PASSES, j=F_ROWS, a=2, u=2)
+            sorted_view = w_sorted[:].rearrange("p h j u (e a x) -> p h u j e a x", e=E_PASS, a=2)
+            for h in range(PASSES):
+                for u in range(2):
+                    nc.vector.tensor_copy(out=sorted_view[:, h, u], in_=raw_view[:, h, u])
+
+            w_grouped = work.tile([P, PASSES, F * PACK], BF16, align_bytes=64)
+            grouped_words = w_grouped[:].bitcast(F32).rearrange("c h (p j x) -> c h j p x", j=2, x=4)
+            for h in range(PASSES):
+                for j_pair in range(2):
+                    flipped = psum_bank.tile([P, 4, P], F32, tag="bank")
+                    for j_low in range(2):
+                        for u in range(2):
+                            nc.tensor.transpose(
+                                flipped[:, 2 * j_low + u, :],
+                                w_sorted[:, h, 2 * j_pair + j_low, u, :].bitcast(F32),
+                                ident_f32[:],
+                            )
+                    nc.scalar.copy(out=grouped_words[:, h, j_pair], in_=flipped[:].rearrange("c x p -> c p x"))
+                nc.vector.quantize_mx(
+                    out=w_codes[:, k, h, :].bitcast(E4M3_X4), scales=w_scales[:, k, h, :], in_=w_grouped[:, h, :]
+                )
+
+        def multiply(i, k):
+            acc = psum_bank.tile([P, F], F32, tag="bank")
+            for h in range(PASSES):
+                tokens = slice(h * P, (h + 1) * P)
+                nc.tensor.matmul_mx(
+                    out=acc[:],
+                    lhsT=gz_codes[:, i, tokens].bitcast(E5M2_X4),
+                    lhsT_scale=gz_scales[:, i, tokens],
+                    rhs=w_codes[:, k, h, :].bitcast(E4M3_X4),
+                    rhs_scale=w_scales[:, k, h, :],
+                    start=(h == 0),
+                    stop=(h == PASSES - 1),
+                )
+            result = results.tile([P, F], F32)
+            if (i * K + k) % VECTOR_TURN == VECTOR_TURN - 1:
+                nc.vector.tensor_copy(out=result[:], in_=acc[:])
+            else:
+                nc.scalar.copy(out=result[:], in_=acc[:])
+            b, n_tile = divmod(i, TILES_PER_BATCH)
+            nc.sync.dma_start(out=out[b, k, n_tile * P : (n_tile + 1) * P, :], in_=result[:])
+
+        quantise_weights(0)
+        for i in range(AHEAD):
+            quantise_gz(i)
+        for step in range(TOKEN_TILES + SKEW * (K - 1)):
+            if step + AHEAD < TOKEN_TILES:
+                quantise_gz(step + AHEAD)
+            for k in range(K):
+                i = step - SKEW * k
+                if 0 <= i < TOKEN_TILES:
+                    multiply(i, k)
+            if step % SKEW == 0 and step // SKEW + 1 < K:
+                quantise_weights(step // SKEW + 1)

@@ -21,7 +21,6 @@ CHUNK_TILES = 4
 CHUNK = CHUNK_TILES * P
 F_ROWS = F // P
 
-SKEW = 2
 AHEAD = 2
 VECTOR_TURN = 6
 
@@ -36,15 +35,14 @@ def tile_dygcn_pb_kernel(tc, x_g, emb, weights_pool, bias_pool, grad_out, out):
     with ExitStack() as stack:
         const = stack.enter_context(tc.tile_pool(name="const", bufs=1))
         keep = stack.enter_context(tc.tile_pool(name="keep", bufs=1))
-        work = stack.enter_context(tc.tile_pool(name="work", bufs=2))
         results = stack.enter_context(tc.tile_pool(name="results", bufs=8))
-        psum_bank = stack.enter_context(tc.psum_pool(name="psum_bank", bufs=4))
-        psum_g = stack.enter_context(tc.psum_pool(name="psum_g", bufs=2))
-        psum_tok = stack.enter_context(tc.psum_pool(name="psum_tok", bufs=2))
+        psum_bank = stack.enter_context(tc.psum_pool(name="psum_bank", bufs=6))
+        psum_g = stack.enter_context(tc.psum_pool(name="psum_g", bufs=AHEAD))
+        stack.enter_context(tc.manual_schedule())
 
         tok_rows = keep.tile([P, TOKEN_TILES, P], BF16)
         nc.vector.memset(tok_rows[:, :, O + E :], 0.0)
-        nc.scalar.dma_start(out=tok_rows[:, :, 0:O], in_=grad_out.rearrange("b (i p) o -> p (b i) o", p=P))
+        nc.sync.dma_start(out=tok_rows[:, :, 0:O], in_=grad_out.rearrange("b (i p) o -> p (b i) o", p=P))
         nc.scalar.dma_start(out=tok_rows[:, :, O : O + E], in_=emb.rearrange("b (i p) e -> p (b i) e", p=P))
 
         w_raw = keep.tile([P, K, E, F_ROWS * O], BF16)
@@ -79,68 +77,84 @@ def tile_dygcn_pb_kernel(tc, x_g, emb, weights_pool, bias_pool, grad_out, out):
 
         tok_cols = keep.tile([P, TOKEN_TILES * P], BF16)
         emb_spread = keep.tile([P, PASSES, TOKEN_TILES * P], BF16)
-        for chunk in range(TOKEN_TILES // CHUNK_TILES):
-            cols = slice(chunk * CHUNK, (chunk + 1) * CHUNK)
-            flipped = psum_tok.tile([P, CHUNK_TILES, P], BF16, tag="tok")
+
+        def flip_tokens(chunk):
+            flipped = psum_bank.tile([P, CHUNK_TILES, P], BF16, tag="bank")
             for i in range(CHUNK_TILES):
                 nc.tensor.transpose(flipped[:, i, :], tok_rows[:, chunk * CHUNK_TILES + i, :], ident_bf16[:])
-            nc.scalar.copy(out=tok_cols[:, cols], in_=flipped[:].rearrange("r i p -> r (i p)"))
-            spread = psum_tok.tile([P, PASSES, CHUNK], BF16, tag="tok")
+            nc.scalar.copy(
+                out=tok_cols[:, chunk * CHUNK : (chunk + 1) * CHUNK], in_=flipped[:].rearrange("r i p -> r (i p)")
+            )
+
+        def spread_emb(chunk):
+            cols = slice(chunk * CHUNK, (chunk + 1) * CHUNK)
+            spread = psum_bank.tile([P, PASSES, CHUNK], BF16, tag="bank")
             for h in range(PASSES):
                 nc.tensor.matmul(
                     out=spread[:, h, :], lhsT=select_e[:, h, :], rhs=tok_cols[:, cols], start=True, stop=True
                 )
             nc.scalar.copy(out=emb_spread[:, :, cols], in_=spread[:])
 
+        gz = keep.tile([P, TOKEN_TILES, PASSES, P, PACK], BF16, align_bytes=64)
         gz_codes = keep.tile([P, TOKEN_TILES, PASSES * P], U32, align_bytes=64)
         gz_scales = keep.tile([P, TOKEN_TILES, PASSES * P], U8, align_bytes=64)
-        w_codes = keep.tile([P, K, PASSES, F], U32, align_bytes=64)
-        w_scales = keep.tile([P, K, PASSES, F], U8, align_bytes=64)
+        g_banks = {}
 
-        def quantise_gz(i):
-            cols = slice(i * P, (i + 1) * P)
+        def spread_g(i):
             g_spread = psum_g.tile([P, PACK, P], F32, tag="g")
             for t in range(PACK):
                 nc.tensor.matmul(
-                    out=g_spread[:, t, :], lhsT=select_o[:, t, :], rhs=tok_cols[:, cols], start=True, stop=True
+                    out=g_spread[:, t, :],
+                    lhsT=select_o[:, t, :],
+                    rhs=tok_cols[:, i * P : (i + 1) * P],
+                    start=True,
+                    stop=True,
                 )
-            gz = work.tile([P, PASSES, P, PACK], BF16, align_bytes=64, bufs=3)
+            g_banks[i] = g_spread
+
+        def gate(i):
             nc.vector.tensor_tensor(
-                out=gz[:],
-                in0=g_spread[:].rearrange("c t n -> c n t").unsqueeze(1).to_broadcast([P, PASSES, P, PACK]),
-                in1=emb_spread[:, :, cols].unsqueeze(3).to_broadcast([P, PASSES, P, PACK]),
+                out=gz[:, i],
+                in0=g_banks[i][:].rearrange("c t n -> c n t").unsqueeze(1).to_broadcast([P, PASSES, P, PACK]),
+                in1=emb_spread[:, :, i * P : (i + 1) * P].unsqueeze(3).to_broadcast([P, PASSES, P, PACK]),
                 op=mult,
             )
+
+        def quantise_gz(i):
             nc.vector.quantize_mx(
                 out=gz_codes[:, i, :].bitcast(E5M2_X4),
                 scales=gz_scales[:, i, :],
-                in_=gz[:].rearrange("c h n t -> c (h n t)"),
+                in_=gz[:, i].rearrange("c h n t -> c (h n t)"),
             )
 
-        def quantise_weights(k):
-            w_sorted = work.tile([P, PASSES, F_ROWS, 2, 2 * P], BF16)
-            raw_view = w_raw[:, k].rearrange("p (h e) (j a u x) -> p h u j e a x", h=PASSES, j=F_ROWS, a=2, u=2)
-            sorted_view = w_sorted[:].rearrange("p h j u (e a x) -> p h u j e a x", e=E_PASS, a=2)
-            for h in range(PASSES):
-                for u in range(2):
-                    nc.vector.tensor_copy(out=sorted_view[:, h, u], in_=raw_view[:, h, u])
+        w_sorted = keep.tile([P, K, PASSES, F_ROWS, 2, 2 * P], BF16)
+        w_grouped = keep.tile([P, K, PASSES, F * PACK], BF16, align_bytes=64)
+        w_codes = keep.tile([P, K, PASSES, F], U32, align_bytes=64)
+        w_scales = keep.tile([P, K, PASSES, F], U8, align_bytes=64)
 
-            w_grouped = work.tile([P, PASSES, F * PACK], BF16, align_bytes=64)
-            grouped_words = w_grouped[:].bitcast(F32).rearrange("c h (p j x) -> c h j p x", j=2, x=4)
-            for h in range(PASSES):
-                for j_pair in range(2):
-                    flipped = psum_bank.tile([P, 4, P], F32, tag="bank")
-                    for j_low in range(2):
-                        for u in range(2):
-                            nc.tensor.transpose(
-                                flipped[:, 2 * j_low + u, :],
-                                w_sorted[:, h, 2 * j_pair + j_low, u, :].bitcast(F32),
-                                ident_f32[:],
-                            )
-                    nc.scalar.copy(out=grouped_words[:, h, j_pair], in_=flipped[:].rearrange("c x p -> c p x"))
-                nc.vector.quantize_mx(
-                    out=w_codes[:, k, h, :].bitcast(E4M3_X4), scales=w_scales[:, k, h, :], in_=w_grouped[:, h, :]
-                )
+        def sort_weights(k, h):
+            raw_view = w_raw[:, k].rearrange("p (h e) (j a u x) -> p h u j e a x", h=PASSES, j=F_ROWS, a=2, u=2)
+            sorted_view = w_sorted[:, k].rearrange("p h j u (e a x) -> p h u j e a x", e=E_PASS, a=2)
+            for u in range(2):
+                nc.vector.tensor_copy(out=sorted_view[:, h, u], in_=raw_view[:, h, u])
+
+        def flip_weights(k, h):
+            grouped_words = w_grouped[:, k, h, :].bitcast(F32).rearrange("c (p j x) -> c j p x", j=2, x=4)
+            for j_pair in range(2):
+                flipped = psum_bank.tile([P, 4, P], F32, tag="bank")
+                for j_low in range(2):
+                    for u in range(2):
+                        nc.tensor.transpose(
+                            flipped[:, 2 * j_low + u, :],
+                            w_sorted[:, k, h, 2 * j_pair + j_low, u, :].bitcast(F32),
+                            ident_f32[:],
+                        )
+                nc.scalar.copy(out=grouped_words[:, j_pair], in_=flipped[:].rearrange("c x p -> c p x"))
+
+        def quantise_weights(k, h):
+            nc.vector.quantize_mx(
+                out=w_codes[:, k, h, :].bitcast(E4M3_X4), scales=w_scales[:, k, h, :], in_=w_grouped[:, k, h, :]
+            )
 
         def multiply(i, k):
             acc = psum_bank.tile([P, F], F32, tag="bank")
@@ -163,15 +177,48 @@ def tile_dygcn_pb_kernel(tc, x_g, emb, weights_pool, bias_pool, grad_out, out):
             b, n_tile = divmod(i, TILES_PER_BATCH)
             nc.sync.dma_start(out=out[b, k, n_tile * P : (n_tile + 1) * P, :], in_=result[:])
 
-        quantise_weights(0)
+        def multiply_new_pairs(r):
+            for k in range(r):
+                multiply(r, k)
+            for i in range(r + 1):
+                multiply(i, r)
+
+        flip_tokens(0)
+        flip_tokens(1)
+        spread_emb(0)
+        spread_emb(1)
         for i in range(AHEAD):
-            quantise_gz(i)
-        for step in range(TOKEN_TILES + SKEW * (K - 1)):
-            if step + AHEAD < TOKEN_TILES:
-                quantise_gz(step + AHEAD)
+            spread_g(i)
+
+        for r in range(K):
+            sort_weights(r, 0)
+            flip_weights(r, 0)
+            if r > 0:
+                quantise_weights(r - 1, 1)
+                multiply_new_pairs(r - 1)
+            gate(r)
+            spread_g(r + AHEAD)
+            sort_weights(r, 1)
+            flip_weights(r, 1)
+            quantise_weights(r, 0)
+            quantise_gz(r)
+        gate(K)
+        quantise_weights(K - 1, 1)
+        gate(K + 1)
+        quantise_gz(K)
+        multiply_new_pairs(K - 1)
+
+        for i in range(K, TOKEN_TILES):
+            new_chunk = (i + AHEAD + 1) % CHUNK_TILES == 0 and i + AHEAD + 1 < TOKEN_TILES
+            if new_chunk:
+                flip_tokens((i + AHEAD + 1) // CHUNK_TILES)
+            if i + AHEAD < TOKEN_TILES:
+                spread_g(i + AHEAD)
+            if i + 1 < TOKEN_TILES:
+                quantise_gz(i + 1)
+            if i + AHEAD < TOKEN_TILES:
+                gate(i + AHEAD)
             for k in range(K):
-                i = step - SKEW * k
-                if 0 <= i < TOKEN_TILES:
-                    multiply(i, k)
-            if step % SKEW == 0 and step // SKEW + 1 < K:
-                quantise_weights(step // SKEW + 1)
+                multiply(i, k)
+            if new_chunk:
+                spread_emb((i + AHEAD + 1) // CHUNK_TILES)

@@ -20,6 +20,7 @@ TILES_PER_BATCH = N // P
 CHUNK_TILES = 4
 CHUNK = CHUNK_TILES * P
 F_ROWS = F // P
+HALVES = K * PASSES
 
 AHEAD = 2
 VECTOR_TURN = 6
@@ -40,10 +41,16 @@ def tile_dygcn_pb_kernel(tc, x_g, emb, weights_pool, bias_pool, grad_out, out):
         psum_g = stack.enter_context(tc.psum_pool(name="psum_g", bufs=AHEAD))
         stack.enter_context(tc.manual_schedule())
 
-        tok_rows = keep.tile([P, TOKEN_TILES, P], BF16)
-        nc.vector.memset(tok_rows[:, :, O + E :], 0.0)
-        nc.sync.dma_start(out=tok_rows[:, :, 0:O], in_=grad_out.rearrange("b (i p) o -> p (b i) o", p=P))
-        nc.scalar.dma_start(out=tok_rows[:, :, O : O + E], in_=emb.rearrange("b (i p) e -> p (b i) e", p=P))
+        g_raw = keep.tile([P, TOKEN_TILES, O], BF16)
+        emb_raw = keep.tile([P, TOKEN_TILES, E], BF16)
+        nc.sync.dma_start(
+            out=g_raw[:].rearrange("p (b sub) o -> p b (sub o)", b=B),
+            in_=grad_out.rearrange("b (p sub) o -> p b (sub o)", sub=TILES_PER_BATCH),
+        )
+        nc.sync.dma_start(
+            out=emb_raw[:].rearrange("p (b sub) e -> p b (sub e)", b=B),
+            in_=emb.rearrange("b (p sub) e -> p b (sub e)", sub=TILES_PER_BATCH),
+        )
 
         w_raw = keep.tile([P, K, E, F_ROWS * O], BF16)
         for k in range(K):
@@ -75,6 +82,10 @@ def tile_dygcn_pb_kernel(tc, x_g, emb, weights_pool, bias_pool, grad_out, out):
                 in_=ident_bf16[:, first : first + E_PASS].unsqueeze(2).to_broadcast([P, E_PASS, P // E_PASS]),
             )
 
+        tok_rows = keep.tile([P, TOKEN_TILES, P], BF16)
+        nc.vector.memset(tok_rows[:, :, O + E :], 0.0)
+        nc.vector.tensor_copy(out=tok_rows[:, :, 0:O], in_=g_raw[:])
+        nc.vector.tensor_copy(out=tok_rows[:, :, O : O + E], in_=emb_raw[:])
         tok_cols = keep.tile([P, TOKEN_TILES * P], BF16)
         emb_spread = keep.tile([P, PASSES, TOKEN_TILES * P], BF16)
 
@@ -174,44 +185,45 @@ def tile_dygcn_pb_kernel(tc, x_g, emb, weights_pool, bias_pool, grad_out, out):
                 nc.vector.tensor_copy(out=result[:], in_=acc[:])
             else:
                 nc.scalar.copy(out=result[:], in_=acc[:])
-            b, n_tile = divmod(i, TILES_PER_BATCH)
-            nc.sync.dma_start(out=out[b, k, n_tile * P : (n_tile + 1) * P, :], in_=result[:])
+            b, sub = divmod(i, TILES_PER_BATCH)
+            rows = out[b, k].rearrange("(p sub) f -> sub p f", sub=TILES_PER_BATCH)
+            nc.sync.dma_start(out=rows[sub], in_=result[:])
 
-        def multiply_new_pairs(r):
-            for k in range(r):
-                multiply(r, k)
-            for i in range(r + 1):
-                multiply(i, r)
+        def multiply_new_pairs(newest):
+            for k in range(newest):
+                multiply(newest, k)
+            for i in range(newest + 1):
+                multiply(i, newest)
 
-        flip_tokens(0)
-        flip_tokens(1)
-        spread_emb(0)
-        spread_emb(1)
+        for chunk in range(TOKEN_TILES // CHUNK_TILES):
+            flip_tokens(chunk)
+        for chunk in range(TOKEN_TILES // CHUNK_TILES):
+            spread_emb(chunk)
         for i in range(AHEAD):
             spread_g(i)
 
-        for r in range(K):
-            sort_weights(r, 0)
-            flip_weights(r, 0)
-            if r > 0:
-                quantise_weights(r - 1, 1)
-                multiply_new_pairs(r - 1)
-            gate(r)
-            spread_g(r + AHEAD)
-            sort_weights(r, 1)
-            flip_weights(r, 1)
-            quantise_weights(r, 0)
-            quantise_gz(r)
+        sort_weights(0, 0)
+        for half in range(HALVES):
+            if half + 1 < HALVES:
+                sort_weights(*divmod(half + 1, PASSES))
+            flip_weights(*divmod(half, PASSES))
+            if half > 0:
+                quantise_weights(*divmod(half - 1, PASSES))
+            k, h = divmod(half, PASSES)
+            if h == 0:
+                if k > 0:
+                    multiply_new_pairs(k - 1)
+                gate(k)
+                spread_g(k + AHEAD)
+            else:
+                quantise_gz(k)
         gate(K)
-        quantise_weights(K - 1, 1)
+        quantise_weights(K - 1, PASSES - 1)
         gate(K + 1)
         quantise_gz(K)
         multiply_new_pairs(K - 1)
 
         for i in range(K, TOKEN_TILES):
-            new_chunk = (i + AHEAD + 1) % CHUNK_TILES == 0 and i + AHEAD + 1 < TOKEN_TILES
-            if new_chunk:
-                flip_tokens((i + AHEAD + 1) // CHUNK_TILES)
             if i + AHEAD < TOKEN_TILES:
                 spread_g(i + AHEAD)
             if i + 1 < TOKEN_TILES:
@@ -220,5 +232,3 @@ def tile_dygcn_pb_kernel(tc, x_g, emb, weights_pool, bias_pool, grad_out, out):
                 gate(i + AHEAD)
             for k in range(K):
                 multiply(i, k)
-            if new_chunk:
-                spread_emb((i + AHEAD + 1) // CHUNK_TILES)

@@ -43,23 +43,33 @@ def tile_dygcn_pb_kernel(tc, x_g, emb, weights_pool, bias_pool, grad_out, out):
 
         g_raw = keep.tile([P, TOKEN_TILES, O], BF16)
         emb_raw = keep.tile([P, TOKEN_TILES, E], BF16)
-        nc.sync.dma_start(
-            out=g_raw[:].rearrange("p (b sub) o -> p b (sub o)", b=B),
-            in_=grad_out.rearrange("b (p sub) o -> p b (sub o)", sub=TILES_PER_BATCH),
-        )
-        nc.sync.dma_start(
-            out=emb_raw[:].rearrange("p (b sub) e -> p b (sub e)", b=B),
-            in_=emb.rearrange("b (p sub) e -> p b (sub e)", sub=TILES_PER_BATCH),
-        )
+
+        def load_tokens(first_b, last_b):
+            tiles = slice(first_b * TILES_PER_BATCH, last_b * TILES_PER_BATCH)
+            nc.sync.dma_start(
+                out=g_raw[:, tiles, :].rearrange("p (b sub) o -> p b (sub o)", sub=TILES_PER_BATCH),
+                in_=grad_out[first_b:last_b].rearrange("b (p sub) o -> p b (sub o)", sub=TILES_PER_BATCH),
+            )
+            nc.sync.dma_start(
+                out=emb_raw[:, tiles, :].rearrange("p (b sub) e -> p b (sub e)", sub=TILES_PER_BATCH),
+                in_=emb[first_b:last_b].rearrange("b (p sub) e -> p b (sub e)", sub=TILES_PER_BATCH),
+            )
 
         w_raw = keep.tile([P, K, E, F_ROWS * O], BF16)
-        for k in range(K):
+
+        def load_weights(k):
             for h in range(PASSES):
                 e_range = slice(h * E_PASS, (h + 1) * E_PASS)
                 nc.sync.dma_start(
                     out=w_raw[:, k, e_range, :],
                     in_=weights_pool[e_range, k].rearrange("e (p j) o -> p e (j o)", j=F_ROWS),
                 )
+
+        load_tokens(0, 1)
+        load_weights(0)
+        load_tokens(1, B)
+        for k in range(1, K):
+            load_weights(k)
 
         ident_bf16 = const.tile([P, P], BF16)
         make_identity(nc, ident_bf16[:])
@@ -84,8 +94,12 @@ def tile_dygcn_pb_kernel(tc, x_g, emb, weights_pool, bias_pool, grad_out, out):
 
         tok_rows = keep.tile([P, TOKEN_TILES, P], BF16)
         nc.vector.memset(tok_rows[:, :, O + E :], 0.0)
-        nc.vector.tensor_copy(out=tok_rows[:, :, 0:O], in_=g_raw[:])
-        nc.vector.tensor_copy(out=tok_rows[:, :, O : O + E], in_=emb_raw[:])
+
+        def lay_tokens(first_b, last_b):
+            tiles = slice(first_b * TILES_PER_BATCH, last_b * TILES_PER_BATCH)
+            nc.vector.tensor_copy(out=tok_rows[:, tiles, 0:O], in_=g_raw[:, tiles, :])
+            nc.vector.tensor_copy(out=tok_rows[:, tiles, O : O + E], in_=emb_raw[:, tiles, :])
+
         tok_cols = keep.tile([P, TOKEN_TILES * P], BF16)
         emb_spread = keep.tile([P, PASSES, TOKEN_TILES * P], BF16)
 
@@ -181,47 +195,67 @@ def tile_dygcn_pb_kernel(tc, x_g, emb, weights_pool, bias_pool, grad_out, out):
                     stop=(h == PASSES - 1),
                 )
             result = results.tile([P, F], F32)
-            if (i * K + k) % VECTOR_TURN == VECTOR_TURN - 1:
-                nc.vector.tensor_copy(out=result[:], in_=acc[:])
-            else:
-                nc.scalar.copy(out=result[:], in_=acc[:])
             b, sub = divmod(i, TILES_PER_BATCH)
             rows = out[b, k].rearrange("(p sub) f -> sub p f", sub=TILES_PER_BATCH)
-            nc.sync.dma_start(out=rows[sub], in_=result[:])
+            pieces = 2 if (i, k) == (TOKEN_TILES - 1, K - 1) else 1
+            for piece in range(pieces):
+                cols = slice(piece * F // pieces, (piece + 1) * F // pieces)
+                if (i * K + k) % VECTOR_TURN == VECTOR_TURN - 1:
+                    nc.vector.tensor_copy(out=result[:, cols], in_=acc[:, cols])
+                else:
+                    nc.scalar.copy(out=result[:, cols], in_=acc[:, cols])
+                nc.sync.dma_start(out=rows[sub][:, cols], in_=result[:, cols])
 
-        def multiply_new_pairs(newest):
-            for k in range(newest):
-                multiply(newest, k)
-            for i in range(newest + 1):
-                multiply(i, newest)
-
-        for chunk in range(TOKEN_TILES // CHUNK_TILES):
-            flip_tokens(chunk)
-        for chunk in range(TOKEN_TILES // CHUNK_TILES):
-            spread_emb(chunk)
+        lay_tokens(0, 1)
+        flip_tokens(0)
+        spread_emb(0)
         for i in range(AHEAD):
             spread_g(i)
-
         sort_weights(0, 0)
-        for half in range(HALVES):
-            if half + 1 < HALVES:
-                sort_weights(*divmod(half + 1, PASSES))
-            flip_weights(*divmod(half, PASSES))
-            if half > 0:
-                quantise_weights(*divmod(half - 1, PASSES))
-            k, h = divmod(half, PASSES)
-            if h == 0:
-                if k > 0:
-                    multiply_new_pairs(k - 1)
-                gate(k)
-                spread_g(k + AHEAD)
-            else:
-                quantise_gz(k)
-        gate(K)
-        quantise_weights(K - 1, PASSES - 1)
-        gate(K + 1)
-        quantise_gz(K)
-        multiply_new_pairs(K - 1)
+        sort_weights(0, 1)
+        flip_weights(0, 0)
+        gate(0)
+        flip_weights(0, 1)
+        lay_tokens(1, B)
+        for chunk in range(1, TOKEN_TILES // CHUNK_TILES):
+            flip_tokens(chunk)
+        sort_weights(1, 0)
+        quantise_weights(0, 0)
+        quantise_gz(0)
+        flip_weights(1, 0)
+        quantise_weights(0, 1)
+        gate(1)
+        multiply(0, 0)
+        spread_g(2)
+        spread_emb(1)
+        sort_weights(1, 1)
+        flip_weights(1, 1)
+        quantise_weights(1, 0)
+        quantise_gz(1)
+        multiply(1, 0)
+        spread_g(3)
+        sort_weights(2, 0)
+        flip_weights(2, 0)
+        quantise_weights(1, 1)
+        gate(2)
+        multiply(0, 1)
+        multiply(1, 1)
+        sort_weights(2, 1)
+        flip_weights(2, 1)
+        quantise_weights(2, 0)
+        quantise_gz(2)
+        gate(3)
+        multiply(2, 0)
+        multiply(2, 1)
+        spread_g(4)
+        spread_emb(2)
+        quantise_weights(2, 1)
+        quantise_gz(3)
+        gate(4)
+        multiply(0, 2)
+        multiply(1, 2)
+        multiply(2, 2)
+        spread_emb(3)
 
         for i in range(K, TOKEN_TILES):
             if i + AHEAD < TOKEN_TILES:

@@ -121,8 +121,10 @@ def tile_dygcn_pb_kernel(tc, x_g, emb, weights_pool, bias_pool, grad_out, out):
             nc.scalar.copy(out=emb_spread[:, :, cols], in_=spread[:])
 
         gz = keep.tile([P, TOKEN_TILES, PASSES, P, PACK], BF16, align_bytes=64)
-        gz_codes = keep.tile([P, TOKEN_TILES, PASSES * P], U32, align_bytes=64)
-        gz_scales = keep.tile([P, TOKEN_TILES, PASSES * P], U8, align_bytes=64)
+        gz_codes_room = keep.tile([P, 64 // 4 + TOKEN_TILES * PASSES * P], U32, align_bytes=256)
+        gz_codes = gz_codes_room[:, 64 // 4 :].rearrange("c (i w) -> c i w", i=TOKEN_TILES)
+        gz_scales_room = keep.tile([P, 192 + TOKEN_TILES * PASSES * P], U8, align_bytes=256)
+        gz_scales = gz_scales_room[:, 192:].rearrange("c (i w) -> c i w", i=TOKEN_TILES)
         g_banks = {}
 
         def spread_g(i):
@@ -154,8 +156,9 @@ def tile_dygcn_pb_kernel(tc, x_g, emb, weights_pool, bias_pool, grad_out, out):
 
         w_sorted = keep.tile([P, K, PASSES, F_ROWS, 2, 2 * P], BF16)
         w_grouped = keep.tile([P, K, PASSES, F * PACK], BF16, align_bytes=64)
-        w_codes = keep.tile([P, K, PASSES, F], U32, align_bytes=64)
-        w_scales = keep.tile([P, K, PASSES, F], U8, align_bytes=64)
+        w_codes = keep.tile([P, K, PASSES, F], U32, align_bytes=256)
+        w_scales_room = keep.tile([P, 128 + K * PASSES * F], U8, align_bytes=256)
+        w_scales = w_scales_room[:, 128:].rearrange("c (k h f) -> c k h f", k=K, h=PASSES)
 
         def sort_weights(k, h):
             raw_view = w_raw[:, k].rearrange("p (h e) (j a u x) -> p h u j e a x", h=PASSES, j=F_ROWS, a=2, u=2)

from contextlib import ExitStack

import concourse.mybir as mybir
from concourse.masks import make_identity

BF16 = mybir.dt.bfloat16
F32 = mybir.dt.float32
U32 = mybir.dt.uint32
U8 = mybir.dt.uint8
E4M3_X4 = mybir.dt.float8_e4m3fn_x4
E5M2_X4 = mybir.dt.float8_e5m2_x4

B, N, F, O, E, K = 4, 512, 512, 64, 16, 3
P = 128
PACK = 4
PASSES = E * O // (P * PACK)
E_PASS = E // PASSES
TOKEN_TILES = B * N // P
TILES_PER_BATCH = N // P
CHUNK_TILES = 4
CHUNK = CHUNK_TILES * P
F_ROWS = F // P
HALVES = K * PASSES

AHEAD = 2
VECTOR_TURN = 6

FLOPS = 2 * B * N * K * F * E * O
BYTES = 2 * (B * N * E + B * N * O + E * K * F * O) + 4 * B * K * N * F


def tile_dygcn_pb_kernel(tc, x_g, emb, weights_pool, bias_pool, grad_out, out):
    nc = tc.nc
    mult = mybir.AluOpType.mult

    with ExitStack() as stack:
        const = stack.enter_context(tc.tile_pool(name="const", bufs=1))
        keep = stack.enter_context(tc.tile_pool(name="keep", bufs=1))
        results = stack.enter_context(tc.tile_pool(name="results", bufs=8))
        psum_bank = stack.enter_context(tc.psum_pool(name="psum_bank", bufs=6))
        psum_g = stack.enter_context(tc.psum_pool(name="psum_g", bufs=AHEAD))
        stack.enter_context(tc.manual_schedule())

        g_raw = keep.tile([P, TOKEN_TILES, O], BF16)
        emb_raw = keep.tile([P, TOKEN_TILES, E], BF16)

        def load_tokens(first_b, last_b):
            tiles = slice(first_b * TILES_PER_BATCH, last_b * TILES_PER_BATCH)
            nc.sync.dma_start(
                out=g_raw[:, tiles, :].rearrange("p (b sub) o -> p b (sub o)", sub=TILES_PER_BATCH),
                in_=grad_out[first_b:last_b].rearrange("b (p sub) o -> p b (sub o)", sub=TILES_PER_BATCH),
            )
            nc.sync.dma_start(
                out=emb_raw[:, tiles, :].rearrange("p (b sub) e -> p b (sub e)", sub=TILES_PER_BATCH),
                in_=emb[first_b:last_b].rearrange("b (p sub) e -> p b (sub e)", sub=TILES_PER_BATCH),
            )

        w_raw = keep.tile([P, K, E, F_ROWS * O], BF16)

        def load_weights(k):
            for h in range(PASSES):
                e_range = slice(h * E_PASS, (h + 1) * E_PASS)
                nc.sync.dma_start(
                    out=w_raw[:, k, e_range, :],
                    in_=weights_pool[e_range, k].rearrange("e (p j) o -> p e (j o)", j=F_ROWS),
                )

        load_tokens(0, 1)
        load_weights(0)
        load_tokens(1, B)
        for k in range(1, K):
            load_weights(k)

        ident_bf16 = const.tile([P, P], BF16)
        make_identity(nc, ident_bf16[:])
        ident_f32 = const.tile([P, P], F32)
        make_identity(nc, ident_f32[:])

        select_o = const.tile([P, PACK, P], BF16)
        ident_by_o = ident_bf16[:, 0:O].rearrange("r (a u q s) -> r u s a q", a=2, u=2, q=8)
        for u in range(2):
            for s in range(2):
                nc.vector.tensor_copy(
                    out=select_o[:, 2 * u + s, :].rearrange("r (e a q) -> r e a q", e=E_PASS, a=2),
                    in_=ident_by_o[:, u, s].unsqueeze(1).to_broadcast([P, E_PASS, 2, 8]),
                )
        select_e = const.tile([P, PASSES, P], BF16)
        for h in range(PASSES):
            first = O + h * E_PASS
            nc.vector.tensor_copy(
                out=select_e[:, h, :].rearrange("r (e x) -> r e x", e=E_PASS),
                in_=ident_bf16[:, first : first + E_PASS].unsqueeze(2).to_broadcast([P, E_PASS, P // E_PASS]),
            )

        tok_rows = keep.tile([P, TOKEN_TILES, P], BF16)
        nc.vector.memset(tok_rows[:, :, O + E :], 0.0)

        def lay_tokens(first_b, last_b):
            tiles = slice(first_b * TILES_PER_BATCH, last_b * TILES_PER_BATCH)
            nc.vector.tensor_copy(out=tok_rows[:, tiles, 0:O], in_=g_raw[:, tiles, :])
            nc.vector.tensor_copy(out=tok_rows[:, tiles, O : O + E], in_=emb_raw[:, tiles, :])

        tok_cols = keep.tile([P, TOKEN_TILES * P], BF16)
        emb_spread = keep.tile([P, PASSES, TOKEN_TILES * P], BF16)

        def flip_tokens(chunk):
            flipped = psum_bank.tile([P, CHUNK_TILES, P], BF16, tag="bank")
            for i in range(CHUNK_TILES):
                nc.tensor.transpose(flipped[:, i, :], tok_rows[:, chunk * CHUNK_TILES + i, :], ident_bf16[:])
            nc.scalar.copy(
                out=tok_cols[:, chunk * CHUNK : (chunk + 1) * CHUNK], in_=flipped[:].rearrange("r i p -> r (i p)")
            )

        def spread_emb(chunk):
            cols = slice(chunk * CHUNK, (chunk + 1) * CHUNK)
            spread = psum_bank.tile([P, PASSES, CHUNK], BF16, tag="bank")
            for h in range(PASSES):
                nc.tensor.matmul(
                    out=spread[:, h, :], lhsT=select_e[:, h, :], rhs=tok_cols[:, cols], start=True, stop=True
                )
            nc.scalar.copy(out=emb_spread[:, :, cols], in_=spread[:])

        gz = keep.tile([P, TOKEN_TILES, PASSES, P, PACK], BF16, align_bytes=64)
        gz_codes_room = keep.tile([P, 64 // 4 + TOKEN_TILES * PASSES * P], U32, align_bytes=256)
        gz_codes = gz_codes_room[:, 64 // 4 :].rearrange("c (i w) -> c i w", i=TOKEN_TILES)
        gz_scales_room = keep.tile([P, 192 + TOKEN_TILES * PASSES * P], U8, align_bytes=256)
        gz_scales = gz_scales_room[:, 192:].rearrange("c (i w) -> c i w", i=TOKEN_TILES)
        g_banks = {}

        def spread_g(i):
            g_spread = psum_g.tile([P, PACK, P], F32, tag="g")
            for t in range(PACK):
                nc.tensor.matmul(
                    out=g_spread[:, t, :],
                    lhsT=select_o[:, t, :],
                    rhs=tok_cols[:, i * P : (i + 1) * P],
                    start=True,
                    stop=True,
                )
            g_banks[i] = g_spread

        def gate(i):
            nc.vector.tensor_tensor(
                out=gz[:, i],
                in0=g_banks[i][:].rearrange("c t n -> c n t").unsqueeze(1).to_broadcast([P, PASSES, P, PACK]),
                in1=emb_spread[:, :, i * P : (i + 1) * P].unsqueeze(3).to_broadcast([P, PASSES, P, PACK]),
                op=mult,
            )

        def quantise_gz(i):
            nc.vector.quantize_mx(
                out=gz_codes[:, i, :].bitcast(E5M2_X4),
                scales=gz_scales[:, i, :],
                in_=gz[:, i].rearrange("c h n t -> c (h n t)"),
            )

        w_sorted = keep.tile([P, K, PASSES, F_ROWS, 2, 2 * P], BF16)
        w_grouped = keep.tile([P, K, PASSES, F * PACK], BF16, align_bytes=64)
        w_codes = keep.tile([P, K, PASSES, F], U32, align_bytes=256)
        w_scales_room = keep.tile([P, 128 + K * PASSES * F], U8, align_bytes=256)
        w_scales = w_scales_room[:, 128:].rearrange("c (k h f) -> c k h f", k=K, h=PASSES)

        def sort_weights(k, h):
            raw_view = w_raw[:, k].rearrange("p (h e) (j a u x) -> p h u j e a x", h=PASSES, j=F_ROWS, a=2, u=2)
            sorted_view = w_sorted[:, k].rearrange("p h j u (e a x) -> p h u j e a x", e=E_PASS, a=2)
            for u in range(2):
                nc.vector.tensor_copy(out=sorted_view[:, h, u], in_=raw_view[:, h, u])

        def flip_weights(k, h):
            grouped_words = w_grouped[:, k, h, :].bitcast(F32).rearrange("c (p j x) -> c j p x", j=2, x=4)
            for j_pair in range(2):
                flipped = psum_bank.tile([P, 4, P], F32, tag="bank")
                for j_low in range(2):
                    for u in range(2):
                        nc.tensor.transpose(
                            flipped[:, 2 * j_low + u, :],
                            w_sorted[:, k, h, 2 * j_pair + j_low, u, :].bitcast(F32),
                            ident_f32[:],
                        )
                nc.scalar.copy(out=grouped_words[:, j_pair], in_=flipped[:].rearrange("c x p -> c p x"))

        def quantise_weights(k, h):
            nc.vector.quantize_mx(
                out=w_codes[:, k, h, :].bitcast(E4M3_X4), scales=w_scales[:, k, h, :], in_=w_grouped[:, k, h, :]
            )

        def multiply(i, k):
            acc = psum_bank.tile([P, F], F32, tag="bank")
            for h in range(PASSES):
                tokens = slice(h * P, (h + 1) * P)
                nc.tensor.matmul_mx(
                    out=acc[:],
                    lhsT=gz_codes[:, i, tokens].bitcast(E5M2_X4),
                    lhsT_scale=gz_scales[:, i, tokens],
                    rhs=w_codes[:, k, h, :].bitcast(E4M3_X4),
                    rhs_scale=w_scales[:, k, h, :],
                    start=(h == 0),
                    stop=(h == PASSES - 1),
                )
            result = results.tile([P, F], F32)
            b, sub = divmod(i, TILES_PER_BATCH)
            rows = out[b, k].rearrange("(p sub) f -> sub p f", sub=TILES_PER_BATCH)
            pieces = 2 if (i, k) == (TOKEN_TILES - 1, K - 1) else 1
            for piece in range(pieces):
                cols = slice(piece * F // pieces, (piece + 1) * F // pieces)
                if (i * K + k) % VECTOR_TURN == VECTOR_TURN - 1:
                    nc.vector.tensor_copy(out=result[:, cols], in_=acc[:, cols])
                else:
                    nc.scalar.copy(out=result[:, cols], in_=acc[:, cols])
                nc.sync.dma_start(out=rows[sub][:, cols], in_=result[:, cols])

        lay_tokens(0, 1)
        flip_tokens(0)
        spread_emb(0)
        for i in range(AHEAD):
            spread_g(i)
        sort_weights(0, 0)
        sort_weights(0, 1)
        flip_weights(0, 0)
        gate(0)
        flip_weights(0, 1)
        lay_tokens(1, B)
        for chunk in range(1, TOKEN_TILES // CHUNK_TILES):
            flip_tokens(chunk)
        sort_weights(1, 0)
        quantise_weights(0, 0)
        quantise_gz(0)
        flip_weights(1, 0)
        quantise_weights(0, 1)
        gate(1)
        multiply(0, 0)
        spread_g(2)
        spread_emb(1)
        sort_weights(1, 1)
        flip_weights(1, 1)
        quantise_weights(1, 0)
        quantise_gz(1)
        multiply(1, 0)
        spread_g(3)
        sort_weights(2, 0)
        flip_weights(2, 0)
        quantise_weights(1, 1)
        gate(2)
        multiply(0, 1)
        multiply(1, 1)
        sort_weights(2, 1)
        flip_weights(2, 1)
        quantise_weights(2, 0)
        quantise_gz(2)
        gate(3)
        multiply(2, 0)
        multiply(2, 1)
        spread_g(4)
        spread_emb(2)
        quantise_weights(2, 1)
        quantise_gz(3)
        gate(4)
        multiply(0, 2)
        multiply(1, 2)
        multiply(2, 2)
        spread_emb(3)

        for i in range(K, TOKEN_TILES):
            if i + AHEAD < TOKEN_TILES:
                spread_g(i + AHEAD)
            if i + 1 < TOKEN_TILES:
                quantise_gz(i + 1)
            if i + AHEAD < TOKEN_TILES:
                gate(i + AHEAD)
            for k in range(K):
                multiply(i, k)
